import numpy as np
import ml_dtypes

BF16 = ml_dtypes.bfloat16


def bf(x):
    return np.asarray(x, np.float32).astype(BF16)


def f32(x):
    return np.asarray(x, np.float32)


def f64(x):
    return np.asarray(x).astype(np.float64)


def striped(idx):
    return np.tile(idx.reshape(-1, 16).T, (8, 1))


C, S, N, KC, D, M, H, R = 1024, 512, 2048, 8, 128, 4, 256, 8


def setup_inputs():
    x = f32(np.maximum(np.random.standard_normal((C, S)), 0.0))
    idx = np.concatenate([np.random.permutation(S)[:H] for _ in range(R)])
    return {"x": x, "offs": striped(idx)}


def reference(x, offs):
    idx = offs[:16].T.reshape(-1)
    xc = f64(x).reshape(KC, D, S)
    xn = xc / np.sqrt((xc * xc).sum(axis=1, keepdims=True))
    z = xn[:, :, idx]
    a = (z * np.tile(xn, (1, 1, M))).sum(axis=1, keepdims=True)
    e = np.exp(a)
    p = e / e.sum(axis=0, keepdims=True)
    return (xn + (z * p).reshape(KC, D, M, S).sum(axis=2)).reshape(C, S)

@@ -1,0 +1,130 @@
+from contextlib import ExitStack
+
+import concourse.mybir as mybir
+from concourse.masks import make_identity
+
+F32 = mybir.dt.float32
+BF16 = mybir.dt.bfloat16
+U16 = mybir.dt.uint16
+FN = mybir.ActivationFunctionType
+ALU = mybir.AluOpType
+
+P = 128
+KC = 8
+S = 512
+M = 4
+NB = S // P
+COLS = S // 16
+
+FLOPS = 3 * KC * P * S + 4 * KC * P * M * S + 3 * KC * M * S
+
+
+def tile_disengcn_kernel(tc, x, offs, out):
+    nc = tc.nc
+    x_caps = x.rearrange("(k d) s -> k d s", d=P)
+    out_caps = out.rearrange("(k d) s -> k d s", d=P)
+
+    with ExitStack() as ctx:
+        held = ctx.enter_context(tc.tile_pool(name="held", bufs=1))
+        norm = ctx.enter_context(tc.tile_pool(name="norm", bufs=2))
+        prod = ctx.enter_context(tc.tile_pool(name="prod", bufs=6))
+        soft = ctx.enter_context(tc.tile_pool(name="soft", bufs=2))
+        weight = ctx.enter_context(tc.tile_pool(name="weight", bufs=12))
+        ps_wide = ctx.enter_context(tc.psum_pool(name="ps_wide", bufs=3))
+        ps_held = ctx.enter_context(tc.psum_pool(name="ps_held", bufs=1))
+
+        offsets = held.tile([P, M * COLS], U16, name="offsets")
+        nc.sync.dma_start(offsets[:], offs)
+        x_sb = [held.tile([P, S], F32, name=f"x{k}") for k in range(KC)]
+        for k in range(KC):
+            queue = nc.scalar if k % 2 == 0 else nc.sync
+            queue.dma_start(x_sb[k][:], x_caps[k])
+
+        warm = held.tile([P, 1], F32, name="warm")
+        nc.vector.memset(warm[:], 1.0)
+        nc.scalar.activation(warm[:], warm[:], FN.Abs_reciprocal_sqrt)
+
+        ones = held.tile([P, P], BF16, name="ones")
+        nc.vector.memset(ones[:], 1.0)
+        p_rows = [held.tile([P, S], F32, name=f"p_rows{i}") for i in range(2)]
+        for i in range(2):
+            nc.vector.memset(p_rows[i][:], 0.0)
+        ident = held.tile([P, P], F32, name="ident")
+        make_identity(nc, ident[:])
+        pick = held.tile([P, KC, P], F32, name="pick")
+        nc.gpsimd.tensor_copy(pick[:], ident[:, 0:KC].unsqueeze(2).to_broadcast([P, KC, P]))
+
+        xn = [held.tile([P, S], F32, name=f"xn{k}") for k in range(KC)]
+        xn_plain = [held.tile([P, S], F32, name=f"xn_plain{k}") for k in range(KC)]
+        for k in range(KC):
+            squares = norm.tile([P, S], BF16, name="squares")
+            nc.scalar.activation(squares[:], x_sb[k][:], FN.Square)
+            length2 = ps_wide.tile([P, S], F32, tag="wide", name="length2")
+            nc.tensor.matmul(length2[:], ones[:], squares[:], start=True, stop=True)
+            inv_length = norm.tile([P, S], F32, name="inv_length")
+            nc.scalar.activation(inv_length[:], length2[:], FN.Abs_reciprocal_sqrt)
+            nc.gpsimd.tensor_tensor(xn[k][:], x_sb[k][:], inv_length[:], ALU.mult)
+            nc.scalar.activation(xn_plain[k][:], xn[k][:], FN.Copy)
+
+        agree_t = [ps_held.tile([P, NB, KC], F32, name=f"agree_t{m}") for m in range(M)]
+        total = [held.tile([P, S], F32, name=f"total{k}") for k in range(KC)]
+        p_wide = {}
+
+        def piece(m):
+            return offsets[:, m * COLS : (m + 1) * COLS]
+
+        def agreements(m):
+            for k in range(KC):
+                q = prod.tile([P, S], F32, name="q")
+                nc.vector.tensor_tensor(q[:], xn[k][:].indirect(piece(m)), xn_plain[k][:], ALU.mult)
+                q_bf = prod.tile([P, S], BF16, name="q_bf")
+                nc.scalar.activation(q_bf[:], q[:], FN.Copy)
+                for b in range(NB):
+                    nc.tensor.matmul(
+                        agree_t[m][:, b, k : k + 1],
+                        q_bf[:, b * P : (b + 1) * P],
+                        ones[:, 0:1],
+                        start=True,
+                        stop=True,
+                    )
+
+        def softmax(m):
+            e_t = soft.tile([P, NB, KC], F32, name="e_t")
+            nc.scalar.activation(e_t[:], agree_t[m][:], FN.Exp)
+            den_t = soft.tile([P, NB], F32, name="den_t")
+            nc.vector.reduce_sum(den_t[:], e_t[:], axis=mybir.AxisListType.X)
+            inv_den_t = soft.tile([P, NB], F32, name="inv_den_t")
+            nc.vector.reciprocal(inv_den_t[:], den_t[:])
+            p_t = soft.tile([P, NB, KC], F32, name="p_t")
+            nc.vector.tensor_tensor(
+                p_t[:], e_t[:], inv_den_t[:].unsqueeze(2).to_broadcast([P, NB, KC]), ALU.mult
+            )
+            p_back = ps_held.tile([KC, S], F32, name="p_back")
+            for b in range(NB):
+                nc.tensor.matmul(
+                    p_back[:, b * P : (b + 1) * P], p_t[:, b, :], ident[:], start=True, stop=True
+                )
+            rows = p_rows[m % 2]
+            nc.scalar.activation(rows[0:KC, :], p_back[:], FN.Copy)
+            for k in range(KC):
+                spread = ps_wide.tile([P, S], F32, tag="wide", name="spread")
+                nc.tensor.matmul(spread[:], pick[:, k, :], rows[:], start=True, stop=True)
+                p_wide[m, k] = weight.tile([P, S], F32, name="p_wide")
+                nc.scalar.activation(p_wide[m, k][:], spread[:], FN.Copy)
+
+        def weighted_sum(m):
+            for k in range(KC):
+                z_p = prod.tile([P, S], F32, name="z_p")
+                nc.vector.tensor_tensor(z_p[:], xn[k][:].indirect(piece(m)), p_wide[m, k][:], ALU.mult)
+                so_far = xn_plain[k] if m == 0 else total[k]
+                nc.gpsimd.tensor_tensor(total[k][:], so_far[:], z_p[:], ALU.add)
+                if m == M - 1:
+                    nc.sync.dma_start(out_caps[k], total[k][:])
+
+        agreements(0)
+        softmax(0)
+        for m in range(1, M):
+            agreements(m)
+            softmax(m)
+            weighted_sum(m - 1)
+        weighted_sum(M - 1)

@@ -29,8 +29,7 @@ def tile_disengcn_kernel(tc, x, offs, out):
         norm = ctx.enter_context(tc.tile_pool(name="norm", bufs=2))
         prod = ctx.enter_context(tc.tile_pool(name="prod", bufs=6))
         soft = ctx.enter_context(tc.tile_pool(name="soft", bufs=2))
-        weight = ctx.enter_context(tc.tile_pool(name="weight", bufs=12))
-        ps_wide = ctx.enter_context(tc.psum_pool(name="ps_wide", bufs=3))
+        ps_wide = ctx.enter_context(tc.psum_pool(name="ps_wide", bufs=6))
         ps_held = ctx.enter_context(tc.psum_pool(name="ps_held", bufs=1))
 
         offsets = held.tile([P, M * COLS], U16, name="offsets")
@@ -43,16 +42,10 @@ def tile_disengcn_kernel(tc, x, offs, out):
         warm = held.tile([P, 1], F32, name="warm")
         nc.vector.memset(warm[:], 1.0)
         nc.scalar.activation(warm[:], warm[:], FN.Abs_reciprocal_sqrt)
-
         ones = held.tile([P, P], BF16, name="ones")
         nc.vector.memset(ones[:], 1.0)
-        p_rows = [held.tile([P, S], F32, name=f"p_rows{i}") for i in range(2)]
-        for i in range(2):
-            nc.vector.memset(p_rows[i][:], 0.0)
         ident = held.tile([P, P], F32, name="ident")
         make_identity(nc, ident[:])
-        pick = held.tile([P, KC, P], F32, name="pick")
-        nc.gpsimd.tensor_copy(pick[:], ident[:, 0:KC].unsqueeze(2).to_broadcast([P, KC, P]))
 
         xn = [held.tile([P, S], F32, name=f"xn{k}") for k in range(KC)]
         xn_plain = [held.tile([P, S], F32, name=f"xn_plain{k}") for k in range(KC)]
@@ -63,12 +56,12 @@ def tile_disengcn_kernel(tc, x, offs, out):
             nc.tensor.matmul(length2[:], ones[:], squares[:], start=True, stop=True)
             inv_length = norm.tile([P, S], F32, name="inv_length")
             nc.scalar.activation(inv_length[:], length2[:], FN.Abs_reciprocal_sqrt)
-            nc.gpsimd.tensor_tensor(xn[k][:], x_sb[k][:], inv_length[:], ALU.mult)
+            nc.vector.tensor_tensor(xn[k][:], x_sb[k][:], inv_length[:], ALU.mult)
             nc.scalar.activation(xn_plain[k][:], xn[k][:], FN.Copy)
 
-        agree_t = [ps_held.tile([P, NB, KC], F32, name=f"agree_t{m}") for m in range(M)]
-        total = [held.tile([P, S], F32, name=f"total{k}") for k in range(KC)]
-        p_wide = {}
+        agree_t = ps_held.tile([P, M, NB, KC], F32, name="agree_t")
+        p_wide = [[held.tile([P, S], F32, name=f"p_wide{m}_{k}") for k in range(KC)] for m in range(M)]
+        total = {}
 
         def piece(m):
             return offsets[:, m * COLS : (m + 1) * COLS]
@@ -81,7 +74,7 @@ def tile_disengcn_kernel(tc, x, offs, out):
                 nc.scalar.activation(q_bf[:], q[:], FN.Copy)
                 for b in range(NB):
                     nc.tensor.matmul(
-                        agree_t[m][:, b, k : k + 1],
+                        agree_t[:, m, b, k : k + 1],
                         q_bf[:, b * P : (b + 1) * P],
                         ones[:, 0:1],
                         start=True,
@@ -90,7 +83,7 @@ def tile_disengcn_kernel(tc, x, offs, out):
 
         def softmax(m):
             e_t = soft.tile([P, NB, KC], F32, name="e_t")
-            nc.scalar.activation(e_t[:], agree_t[m][:], FN.Exp)
+            nc.scalar.activation(e_t[:], agree_t[:, m], FN.Exp)
             den_t = soft.tile([P, NB], F32, name="den_t")
             nc.vector.reduce_sum(den_t[:], e_t[:], axis=mybir.AxisListType.X)
             inv_den_t = soft.tile([P, NB], F32, name="inv_den_t")
@@ -104,27 +97,35 @@ def tile_disengcn_kernel(tc, x, offs, out):
                 nc.tensor.matmul(
                     p_back[:, b * P : (b + 1) * P], p_t[:, b, :], ident[:], start=True, stop=True
                 )
-            rows = p_rows[m % 2]
-            nc.scalar.activation(rows[0:KC, :], p_back[:], FN.Copy)
+            p_rows = soft.tile([KC, S], F32, name="p_rows")
+            nc.scalar.activation(p_rows[:], p_back[:], FN.Copy)
+            first_row = (KC - 1) * P + m * KC
+            nc.sync.dma_start(out[first_row : first_row + KC, :], p_rows[:])
             for k in range(KC):
-                spread = ps_wide.tile([P, S], F32, tag="wide", name="spread")
-                nc.tensor.matmul(spread[:], pick[:, k, :], rows[:], start=True, stop=True)
-                p_wide[m, k] = weight.tile([P, S], F32, name="p_wide")
-                nc.scalar.activation(p_wide[m, k][:], spread[:], FN.Copy)
+                nc.sync.dma_start(p_wide[m][k][:], out[first_row + k, :].partition_broadcast(P))
 
-        def weighted_sum(m):
-            for k in range(KC):
-                z_p = prod.tile([P, S], F32, name="z_p")
-                nc.vector.tensor_tensor(z_p[:], xn[k][:].indirect(piece(m)), p_wide[m, k][:], ALU.mult)
-                so_far = xn_plain[k] if m == 0 else total[k]
-                nc.gpsimd.tensor_tensor(total[k][:], so_far[:], z_p[:], ALU.add)
-                if m == M - 1:
-                    nc.sync.dma_start(out_caps[k], total[k][:])
+        def weighted_sum(m, k):
+            if m == 0:
+                total[k] = ps_wide.tile([P, S], F32, tag="wide", name="total")
+                nc.tensor.matmul(total[k][:], ident[:], xn_plain[k][:], start=True, stop=False)
+            z_p = prod.tile([P, S], F32, name="z_p")
+            nc.vector.tensor_tensor(z_p[:], xn[k][:].indirect(piece(m)), p_wide[m][k][:], ALU.mult)
+            nc.tensor.matmul(total[k][:], ident[:], z_p[:], start=False, stop=(m == M - 1))
+            if m == M - 1:
+                result = norm.tile([P, S], F32, name="result")
+                nc.scalar.activation(result[:], total[k][:], FN.Copy)
+                nc.sync.dma_start(out_caps[k], result[:])
 
+        half = KC // 2
         agreements(0)
         softmax(0)
         for m in range(1, M):
             agreements(m)
             softmax(m)
-            weighted_sum(m - 1)
-        weighted_sum(M - 1)
+            for k in range(half):
+                weighted_sum(m - 1, k)
+        for k in range(half):
+            weighted_sum(M - 1, k)
+        for k in range(half, KC):
+            for m in range(M):
+                weighted_sum(m, k)

@@ -15,6 +15,8 @@ S = 512
 M = 4
 NB = S // P
 COLS = S // 16
+EARLY = 6
+N_PRODUCTS = 6
 
 FLOPS = 3 * KC * P * S + 4 * KC * P * M * S + 3 * KC * M * S
 
@@ -26,10 +28,9 @@ def tile_disengcn_kernel(tc, x, offs, out):
 
     with ExitStack() as ctx:
         held = ctx.enter_context(tc.tile_pool(name="held", bufs=1))
-        norm = ctx.enter_context(tc.tile_pool(name="norm", bufs=2))
-        prod = ctx.enter_context(tc.tile_pool(name="prod", bufs=6))
-        soft = ctx.enter_context(tc.tile_pool(name="soft", bufs=2))
-        ps_wide = ctx.enter_context(tc.psum_pool(name="ps_wide", bufs=6))
+        work = ctx.enter_context(tc.tile_pool(name="work", bufs=2))
+        casts = ctx.enter_context(tc.tile_pool(name="casts", bufs=3))
+        ps_total = ctx.enter_context(tc.psum_pool(name="ps_total", bufs=EARLY))
         ps_held = ctx.enter_context(tc.psum_pool(name="ps_held", bufs=1))
 
         offsets = held.tile([P, M * COLS], U16, name="offsets")
@@ -47,85 +48,113 @@ def tile_disengcn_kernel(tc, x, offs, out):
         ident = held.tile([P, P], F32, name="ident")
         make_identity(nc, ident[:])
 
+        sums_t = ps_held.tile([P, M + 1, NB, KC], F32, name="sums_t")
+
+        def sum_over_d(dest, k, values):
+            for b in range(NB):
+                nc.tensor.matmul(
+                    dest[:, b, k : k + 1],
+                    values[:, b * P : (b + 1) * P],
+                    ones[:, 0:1],
+                    start=True,
+                    stop=True,
+                )
+
         xn = [held.tile([P, S], F32, name=f"xn{k}") for k in range(KC)]
-        xn_plain = [held.tile([P, S], F32, name=f"xn_plain{k}") for k in range(KC)]
         for k in range(KC):
-            squares = norm.tile([P, S], BF16, name="squares")
+            squares = work.tile([P, S], BF16, name="squares")
             nc.scalar.activation(squares[:], x_sb[k][:], FN.Square)
-            length2 = ps_wide.tile([P, S], F32, tag="wide", name="length2")
+            length2 = ps_held.tile([P, S], F32, tag="short", name="length2")
             nc.tensor.matmul(length2[:], ones[:], squares[:], start=True, stop=True)
-            inv_length = norm.tile([P, S], F32, name="inv_length")
+            sum_over_d(sums_t[:, M], k, squares)
+            inv_length = work.tile([P, S], F32, name="inv_length")
             nc.scalar.activation(inv_length[:], length2[:], FN.Abs_reciprocal_sqrt)
             nc.vector.tensor_tensor(xn[k][:], x_sb[k][:], inv_length[:], ALU.mult)
-            nc.scalar.activation(xn_plain[k][:], xn[k][:], FN.Copy)
+        inv_length_t = held.tile([P, NB, KC], F32, name="inv_length_t")
+        nc.scalar.activation(inv_length_t[:], sums_t[:, M], FN.Abs_reciprocal_sqrt)
 
-        agree_t = ps_held.tile([P, M, NB, KC], F32, name="agree_t")
         p_wide = [[held.tile([P, S], F32, name=f"p_wide{m}_{k}") for k in range(KC)] for m in range(M)]
-        total = {}
+        total_t = {}
+
+        products = [held.tile([P, S], F32, name=f"product{i}") for i in range(N_PRODUCTS)]
+        taken = []
+
+        def next_product():
+            taken.append(products[len(taken) % N_PRODUCTS])
+            return taken[-1]
 
         def piece(m):
             return offsets[:, m * COLS : (m + 1) * COLS]
 
         def agreements(m):
             for k in range(KC):
-                q = prod.tile([P, S], F32, name="q")
-                nc.vector.tensor_tensor(q[:], xn[k][:].indirect(piece(m)), xn_plain[k][:], ALU.mult)
-                q_bf = prod.tile([P, S], BF16, name="q_bf")
+                q = next_product()
+                nc.vector.tensor_tensor(q[:], xn[k][:].indirect(piece(m)), x_sb[k][:], ALU.mult)
+                q_bf = casts.tile([P, S], BF16, name="q_bf")
                 nc.scalar.activation(q_bf[:], q[:], FN.Copy)
-                for b in range(NB):
-                    nc.tensor.matmul(
-                        agree_t[:, m, b, k : k + 1],
-                        q_bf[:, b * P : (b + 1) * P],
-                        ones[:, 0:1],
-                        start=True,
-                        stop=True,
-                    )
+                sum_over_d(sums_t[:, m], k, q_bf)
 
         def softmax(m):
-            e_t = soft.tile([P, NB, KC], F32, name="e_t")
-            nc.scalar.activation(e_t[:], agree_t[:, m], FN.Exp)
-            den_t = soft.tile([P, NB], F32, name="den_t")
+            a_t = work.tile([P, NB, KC], F32, name="a_t")
+            nc.vector.tensor_tensor(a_t[:], sums_t[:, m], inv_length_t[:], ALU.mult)
+            e_t = work.tile([P, NB, KC], F32, name="e_t")
+            nc.scalar.activation(e_t[:], a_t[:], FN.Exp)
+            den_t = work.tile([P, NB], F32, name="den_t")
             nc.vector.reduce_sum(den_t[:], e_t[:], axis=mybir.AxisListType.X)
-            inv_den_t = soft.tile([P, NB], F32, name="inv_den_t")
+            inv_den_t = work.tile([P, NB], F32, name="inv_den_t")
             nc.vector.reciprocal(inv_den_t[:], den_t[:])
-            p_t = soft.tile([P, NB, KC], F32, name="p_t")
+            p_t = work.tile([P, NB, KC], F32, name="p_t")
             nc.vector.tensor_tensor(
                 p_t[:], e_t[:], inv_den_t[:].unsqueeze(2).to_broadcast([P, NB, KC]), ALU.mult
             )
-            p_back = ps_held.tile([KC, S], F32, name="p_back")
+            p_back = ps_held.tile([KC, S], F32, tag="short", name="p_back")
             for b in range(NB):
-                nc.tensor.matmul(
-                    p_back[:, b * P : (b + 1) * P], p_t[:, b, :], ident[:], start=True, stop=True
-                )
-            p_rows = soft.tile([KC, S], F32, name="p_rows")
+                nc.tensor.transpose(p_back[:, b * P : (b + 1) * P], p_t[:, b, :], ident[:])
+            p_rows = work.tile([KC, S], F32, name="p_rows")
             nc.scalar.activation(p_rows[:], p_back[:], FN.Copy)
             first_row = (KC - 1) * P + m * KC
             nc.sync.dma_start(out[first_row : first_row + KC, :], p_rows[:])
             for k in range(KC):
                 nc.sync.dma_start(p_wide[m][k][:], out[first_row + k, :].partition_broadcast(P))
 
+        def add_to_total(k, values, first, last):
+            for b in range(NB):
+                nc.tensor.matmul(
+                    total_t[k][:, b, :],
+                    values[:, b * P : (b + 1) * P],
+                    ident[:],
+                    is_transpose=True,
+                    start=(first and b == 0),
+                    stop=(last and b == NB - 1),
+                )
+
+        def open_total(k):
+            total_t[k] = ps_total.tile([P, NB, P], F32, name="total_t")
+            add_to_total(k, xn[k], True, False)
+
         def weighted_sum(m, k):
-            if m == 0:
-                total[k] = ps_wide.tile([P, S], F32, tag="wide", name="total")
-                nc.tensor.matmul(total[k][:], ident[:], xn_plain[k][:], start=True, stop=False)
-            z_p = prod.tile([P, S], F32, name="z_p")
+            z_p = next_product()
             nc.vector.tensor_tensor(z_p[:], xn[k][:].indirect(piece(m)), p_wide[m][k][:], ALU.mult)
-            nc.tensor.matmul(total[k][:], ident[:], z_p[:], start=False, stop=(m == M - 1))
+            add_to_total(k, z_p, False, m == M - 1)
             if m == M - 1:
-                result = norm.tile([P, S], F32, name="result")
-                nc.scalar.activation(result[:], total[k][:], FN.Copy)
+                result_t = work.tile([P, NB, P], F32, name="result_t")
+                nc.scalar.activation(result_t[:], total_t[k][:], FN.Copy)
+                turned = ps_held.tile([P, S], F32, tag="short", name="turned")
+                for b in range(NB):
+                    nc.tensor.transpose(turned[:, b * P : (b + 1) * P], result_t[:, b, :], ident[:])
+                result = work.tile([P, S], F32, name="result")
+                nc.scalar.activation(result[:], turned[:], FN.Copy)
                 nc.sync.dma_start(out_caps[k], result[:])
 
-        half = KC // 2
-        agreements(0)
-        softmax(0)
-        for m in range(1, M):
+        for k in range(EARLY):
+            open_total(k)
+        for m in range(M):
             agreements(m)
             softmax(m)
-            for k in range(half):
-                weighted_sum(m - 1, k)
-        for k in range(half):
-            weighted_sum(M - 1, k)
-        for k in range(half, KC):
+        for m in range(M):
+            for k in range(EARLY):
+                weighted_sum(m, k)
+        for k in range(EARLY, KC):
+            open_total(k)
             for m in range(M):
                 weighted_sum(m, k)

@@ -15,8 +15,9 @@ S = 512
 M = 4
 NB = S // P
 COLS = S // 16
-EARLY = 6
-N_PRODUCTS = 6
+PSUM_BANKS = 8
+EARLY = PSUM_BANKS - 2
+N_PRODUCTS = 3
 
 FLOPS = 3 * KC * P * S + 4 * KC * P * M * S + 3 * KC * M * S
 
@@ -29,7 +30,7 @@ def tile_disengcn_kernel(tc, x, offs, out):
     with ExitStack() as ctx:
         held = ctx.enter_context(tc.tile_pool(name="held", bufs=1))
         work = ctx.enter_context(tc.tile_pool(name="work", bufs=2))
-        casts = ctx.enter_context(tc.tile_pool(name="casts", bufs=3))
+        casts = ctx.enter_context(tc.tile_pool(name="casts", bufs=N_PRODUCTS))
         ps_total = ctx.enter_context(tc.psum_pool(name="ps_total", bufs=EARLY))
         ps_held = ctx.enter_context(tc.psum_pool(name="ps_held", bufs=1))
 
@@ -37,8 +38,7 @@ def tile_disengcn_kernel(tc, x, offs, out):
         nc.sync.dma_start(offsets[:], offs)
         x_sb = [held.tile([P, S], F32, name=f"x{k}") for k in range(KC)]
         for k in range(KC):
-            queue = nc.scalar if k % 2 == 0 else nc.sync
-            queue.dma_start(x_sb[k][:], x_caps[k])
+            nc.sync.dma_start(x_sb[k][:], x_caps[k])
 
         warm = held.tile([P, 1], F32, name="warm")
         nc.vector.memset(warm[:], 1.0)
@@ -73,9 +73,6 @@ def tile_disengcn_kernel(tc, x, offs, out):
         inv_length_t = held.tile([P, NB, KC], F32, name="inv_length_t")
         nc.scalar.activation(inv_length_t[:], sums_t[:, M], FN.Abs_reciprocal_sqrt)
 
-        p_wide = [[held.tile([P, S], F32, name=f"p_wide{m}_{k}") for k in range(KC)] for m in range(M)]
-        total_t = {}
-
         products = [held.tile([P, S], F32, name=f"product{i}") for i in range(N_PRODUCTS)]
         taken = []
 
@@ -88,11 +85,17 @@ def tile_disengcn_kernel(tc, x, offs, out):
 
         def agreements(m):
             for k in range(KC):
-                q = next_product()
-                nc.vector.tensor_tensor(q[:], xn[k][:].indirect(piece(m)), x_sb[k][:], ALU.mult)
+                q_long = next_product()
+                nc.vector.tensor_tensor(
+                    q_long[:], xn[k][:].indirect(piece(m)), x_sb[k][:], ALU.mult
+                )
                 q_bf = casts.tile([P, S], BF16, name="q_bf")
-                nc.scalar.activation(q_bf[:], q[:], FN.Copy)
+                nc.scalar.activation(q_bf[:], q_long[:], FN.Copy)
                 sum_over_d(sums_t[:, m], k, q_bf)
+
+        p_wide = [
+            [held.tile([P, S], F32, name=f"p_wide{m}_{k}") for k in range(KC)] for m in range(M)
+        ]
 
         def softmax(m):
             a_t = work.tile([P, NB, KC], F32, name="a_t")
@@ -117,6 +120,8 @@ def tile_disengcn_kernel(tc, x, offs, out):
             for k in range(KC):
                 nc.sync.dma_start(p_wide[m][k][:], out[first_row + k, :].partition_broadcast(P))
 
+        total_t = {}
+
         def add_to_total(k, values, first, last):
             for b in range(NB):
                 nc.tensor.matmul(
@@ -132,19 +137,22 @@ def tile_disengcn_kernel(tc, x, offs, out):
             total_t[k] = ps_total.tile([P, NB, P], F32, name="total_t")
             add_to_total(k, xn[k], True, False)
 
+        def store_total(k):
+            result_t = work.tile([P, NB, P], F32, name="result_t")
+            nc.scalar.activation(result_t[:], total_t[k][:], FN.Copy)
+            turned = ps_held.tile([P, S], F32, tag="short", name="turned")
+            for b in range(NB):
+                nc.tensor.transpose(turned[:, b * P : (b + 1) * P], result_t[:, b, :], ident[:])
+            result = work.tile([P, S], F32, name="result")
+            nc.scalar.activation(result[:], turned[:], FN.Copy)
+            nc.sync.dma_start(out_caps[k], result[:])
+
         def weighted_sum(m, k):
             z_p = next_product()
             nc.vector.tensor_tensor(z_p[:], xn[k][:].indirect(piece(m)), p_wide[m][k][:], ALU.mult)
             add_to_total(k, z_p, False, m == M - 1)
             if m == M - 1:
-                result_t = work.tile([P, NB, P], F32, name="result_t")
-                nc.scalar.activation(result_t[:], total_t[k][:], FN.Copy)
-                turned = ps_held.tile([P, S], F32, tag="short", name="turned")
-                for b in range(NB):
-                    nc.tensor.transpose(turned[:, b * P : (b + 1) * P], result_t[:, b, :], ident[:])
-                result = work.tile([P, S], F32, name="result")
-                nc.scalar.activation(result[:], turned[:], FN.Copy)
-                nc.sync.dma_start(out_caps[k], result[:])
+                store_total(k)
 
         for k in range(EARLY):
             open_total(k)

@@ -101,15 +101,18 @@ def tile_disengcn_kernel(tc, x, offs, out):
             a_t = work.tile([P, NB, KC], F32, name="a_t")
             nc.vector.tensor_tensor(a_t[:], sums_t[:, m], inv_length_t[:], ALU.mult)
             e_t = work.tile([P, NB, KC], F32, name="e_t")
-            nc.scalar.activation(e_t[:], a_t[:], FN.Exp)
             den_t = work.tile([P, NB], F32, name="den_t")
-            nc.vector.reduce_sum(den_t[:], e_t[:], axis=mybir.AxisListType.X)
+            for b in range(NB):
+                nc.scalar.activation(
+                    e_t[:, b, :], a_t[:, b, :], FN.Exp, accum_out=den_t[:, b : b + 1]
+                )
             inv_den_t = work.tile([P, NB], F32, name="inv_den_t")
             nc.vector.reciprocal(inv_den_t[:], den_t[:])
             p_t = work.tile([P, NB, KC], F32, name="p_t")
-            nc.vector.tensor_tensor(
-                p_t[:], e_t[:], inv_den_t[:].unsqueeze(2).to_broadcast([P, NB, KC]), ALU.mult
-            )
+            for b in range(NB):
+                nc.scalar.activation(
+                    p_t[:, b, :], e_t[:, b, :], FN.Copy, scale=inv_den_t[:, b : b + 1]
+                )
             p_back = ps_held.tile([KC, S], F32, tag="short", name="p_back")
             for b in range(NB):
                 nc.tensor.transpose(p_back[:, b * P : (b + 1) * P], p_t[:, b, :], ident[:])

@@ -140,22 +140,16 @@ def tile_disengcn_kernel(tc, x, offs, out):
             total_t[k] = ps_total.tile([P, NB, P], F32, name="total_t")
             add_to_total(k, xn[k], True, False)
 
-        def store_total(k):
+        def turn_back(k, turned):
             result_t = work.tile([P, NB, P], F32, name="result_t")
             nc.scalar.activation(result_t[:], total_t[k][:], FN.Copy)
-            turned = ps_held.tile([P, S], F32, tag="short", name="turned")
             for b in range(NB):
                 nc.tensor.transpose(turned[:, b * P : (b + 1) * P], result_t[:, b, :], ident[:])
-            result = work.tile([P, S], F32, name="result")
-            nc.scalar.activation(result[:], turned[:], FN.Copy)
-            nc.sync.dma_start(out_caps[k], result[:])
 
-        def weighted_sum(m, k):
+        def weighted(m, k):
             z_p = next_product()
             nc.vector.tensor_tensor(z_p[:], xn[k][:].indirect(piece(m)), p_wide[m][k][:], ALU.mult)
-            add_to_total(k, z_p, False, m == M - 1)
-            if m == M - 1:
-                store_total(k)
+            return z_p
 
         for k in range(EARLY):
             open_total(k)
@@ -164,8 +158,24 @@ def tile_disengcn_kernel(tc, x, offs, out):
             softmax(m)
         for m in range(M):
             for k in range(EARLY):
-                weighted_sum(m, k)
-        for k in range(EARLY, KC):
+                add_to_total(k, weighted(m, k), False, m == M - 1)
+                if m == M - 1:
+                    turned = ps_held.tile([P, S], F32, tag="short", name="turned")
+                    turn_back(k, turned)
+                    result = work.tile([P, S], F32, name="result")
+                    nc.scalar.activation(result[:], turned[:], FN.Copy)
+                    nc.sync.dma_start(out_caps[k], result[:])
+        late = range(EARLY, KC)
+        all_but_last = {}
+        for k in late:
             open_total(k)
-            for m in range(M):
-                weighted_sum(m, k)
+            for m in range(M - 1):
+                add_to_total(k, weighted(m, k), False, m == M - 2)
+            all_but_last[k] = ps_total.tile([P, S], F32, tag="total_t", name="all_but_last")
+            turn_back(k, all_but_last[k])
+        for k in late:
+            finished = work.tile([P, S], F32, name="finished")
+            nc.vector.tensor_tensor(
+                finished[:], weighted(M - 1, k)[:], all_but_last[k][:], ALU.add
+            )
+            nc.sync.dma_start(out_caps[k], finished[:])

@@ -64,7 +64,7 @@ def tile_disengcn_kernel(tc, x, offs, out):
         for k in range(KC):
             squares = work.tile([P, S], BF16, name="squares")
             nc.scalar.activation(squares[:], x_sb[k][:], FN.Square)
-            length2 = ps_held.tile([P, S], F32, tag="short", name="length2")
+            length2 = ps_total.tile([P, S], F32, tag="total_t", name="length2")
             nc.tensor.matmul(length2[:], ones[:], squares[:], start=True, stop=True)
             sum_over_d(sums_t[:, M], k, squares)
             inv_length = work.tile([P, S], F32, name="inv_length")
@@ -93,9 +93,7 @@ def tile_disengcn_kernel(tc, x, offs, out):
                 nc.scalar.activation(q_bf[:], q_long[:], FN.Copy)
                 sum_over_d(sums_t[:, m], k, q_bf)
 
-        p_wide = [
-            [held.tile([P, S], F32, name=f"p_wide{m}_{k}") for k in range(KC)] for m in range(M)
-        ]
+        p_wide = [held.tile([P, KC, S], F32, name=f"p_wide{m}") for m in range(M)]
 
         def softmax(m):
             a_t = work.tile([P, NB, KC], F32, name="a_t")
@@ -119,9 +117,12 @@ def tile_disengcn_kernel(tc, x, offs, out):
             p_rows = work.tile([KC, S], F32, name="p_rows")
             nc.scalar.activation(p_rows[:], p_back[:], FN.Copy)
             first_row = (KC - 1) * P + m * KC
-            nc.sync.dma_start(out[first_row : first_row + KC, :], p_rows[:])
-            for k in range(KC):
-                nc.sync.dma_start(p_wide[m][k][:], out[first_row + k, :].partition_broadcast(P))
+            parked = out[first_row : first_row + KC, :]
+            nc.sync.dma_start(parked, p_rows[:])
+            nc.sync.dma_start(
+                p_wide[m][:].rearrange("d k s -> d (k s)"),
+                parked.rearrange("k s -> (k s)").partition_broadcast(P),
+            )
 
         total_t = {}
 
@@ -148,7 +149,7 @@ def tile_disengcn_kernel(tc, x, offs, out):
 
         def weighted(m, k):
             z_p = next_product()
-            nc.vector.tensor_tensor(z_p[:], xn[k][:].indirect(piece(m)), p_wide[m][k][:], ALU.mult)
+            nc.vector.tensor_tensor(z_p[:], xn[k][:].indirect(piece(m)), p_wide[m][:, k, :], ALU.mult)
             return z_p
 
         for k in range(EARLY):

@@ -43,35 +43,39 @@ def tile_disengcn_kernel(tc, x, offs, out):
         warm = held.tile([P, 1], F32, name="warm")
         nc.vector.memset(warm[:], 1.0)
         nc.scalar.activation(warm[:], warm[:], FN.Abs_reciprocal_sqrt)
-        ones = held.tile([P, P], BF16, name="ones")
+        ones = held.tile([P, 1], BF16, name="ones")
         nc.vector.memset(ones[:], 1.0)
         ident = held.tile([P, P], F32, name="ident")
         make_identity(nc, ident[:])
 
-        sums_t = ps_held.tile([P, M + 1, NB, KC], F32, name="sums_t")
-
-        def sum_over_d(dest, k, values):
+        def sum_over_d(dest, values):
             for b in range(NB):
                 nc.tensor.matmul(
-                    dest[:, b, k : k + 1],
+                    dest[:, b : b + 1],
                     values[:, b * P : (b + 1) * P],
-                    ones[:, 0:1],
+                    ones[:],
                     start=True,
                     stop=True,
                 )
 
         xn = [held.tile([P, S], F32, name=f"xn{k}") for k in range(KC)]
+        inv_length_t = held.tile([P, KC, NB], F32, name="inv_length_t")
         for k in range(KC):
             squares = work.tile([P, S], BF16, name="squares")
             nc.scalar.activation(squares[:], x_sb[k][:], FN.Square)
-            length2 = ps_total.tile([P, S], F32, tag="total_t", name="length2")
-            nc.tensor.matmul(length2[:], ones[:], squares[:], start=True, stop=True)
-            sum_over_d(sums_t[:, M], k, squares)
-            inv_length = work.tile([P, S], F32, name="inv_length")
-            nc.scalar.activation(inv_length[:], length2[:], FN.Abs_reciprocal_sqrt)
+            length2_t = ps_total.tile([P, NB], F32, tag="total_t", name="length2_t")
+            sum_over_d(length2_t, squares)
+            nc.scalar.activation(inv_length_t[:, k, :], length2_t[:], FN.Abs_reciprocal_sqrt)
+            inv_length = ps_total.tile([P, S], F32, tag="total_t", name="inv_length")
+            for b in range(NB):
+                nc.tensor.transpose(
+                    inv_length[:, b * P : (b + 1) * P],
+                    inv_length_t[:, k, b : b + 1].to_broadcast([P, P]),
+                    ident[:],
+                )
             nc.vector.tensor_tensor(xn[k][:], x_sb[k][:], inv_length[:], ALU.mult)
-        inv_length_t = held.tile([P, NB, KC], F32, name="inv_length_t")
-        nc.scalar.activation(inv_length_t[:], sums_t[:, M], FN.Abs_reciprocal_sqrt)
+
+        sums_t = ps_held.tile([P, M, NB, KC], F32, name="sums_t")
 
         products = [held.tile([P, S], F32, name=f"product{i}") for i in range(N_PRODUCTS)]
         taken = []
@@ -91,13 +95,15 @@ def tile_disengcn_kernel(tc, x, offs, out):
                 )
                 q_bf = casts.tile([P, S], BF16, name="q_bf")
                 nc.scalar.activation(q_bf[:], q_long[:], FN.Copy)
-                sum_over_d(sums_t[:, m], k, q_bf)
+                sum_over_d(sums_t[:, m, :, k], q_bf)
 
         p_wide = [held.tile([P, KC, S], F32, name=f"p_wide{m}") for m in range(M)]
 
         def softmax(m):
             a_t = work.tile([P, NB, KC], F32, name="a_t")
-            nc.vector.tensor_tensor(a_t[:], sums_t[:, m], inv_length_t[:], ALU.mult)
+            nc.vector.tensor_tensor(
+                a_t[:], sums_t[:, m], inv_length_t[:].rearrange("p k b -> p b k"), ALU.mult
+            )
             e_t = work.tile([P, NB, KC], F32, name="e_t")
             den_t = work.tile([P, NB], F32, name="den_t")
             for b in range(NB):

@@ -35,9 +35,13 @@ def tile_disengcn_kernel(tc, x, offs, out):
         ps_held = ctx.enter_context(tc.psum_pool(name="ps_held", bufs=1))
 
         offsets = held.tile([P, M * COLS], U16, name="offsets")
-        nc.sync.dma_start(offsets[:], offs)
         x_sb = [held.tile([P, S], F32, name=f"x{k}") for k in range(KC)]
-        for k in range(KC):
+        for first in range(0, S, S // 2):
+            nc.sync.dma_start(
+                x_sb[0][:, first : first + S // 2], x_caps[0][:, first : first + S // 2]
+            )
+        nc.sync.dma_start(offsets[:], offs)
+        for k in range(1, KC):
             nc.sync.dma_start(x_sb[k][:], x_caps[k])
 
         warm = held.tile([P, 1], F32, name="warm")
@@ -48,8 +52,8 @@ def tile_disengcn_kernel(tc, x, offs, out):
         ident = held.tile([P, P], F32, name="ident")
         make_identity(nc, ident[:])
 
-        def sum_over_d(dest, values):
-            for b in range(NB):
+        def sum_over_d(dest, values, n_blocks):
+            for b in range(n_blocks):
                 nc.tensor.matmul(
                     dest[:, b : b + 1],
                     values[:, b * P : (b + 1) * P],
@@ -60,20 +64,30 @@ def tile_disengcn_kernel(tc, x, offs, out):
 
         xn = [held.tile([P, S], F32, name=f"xn{k}") for k in range(KC)]
         inv_length_t = held.tile([P, KC, NB], F32, name="inv_length_t")
-        for k in range(KC):
-            squares = work.tile([P, S], BF16, name="squares")
-            nc.scalar.activation(squares[:], x_sb[k][:], FN.Square)
-            length2_t = ps_total.tile([P, NB], F32, tag="total_t", name="length2_t")
-            sum_over_d(length2_t, squares)
-            nc.scalar.activation(inv_length_t[:, k, :], length2_t[:], FN.Abs_reciprocal_sqrt)
-            inv_length = ps_total.tile([P, S], F32, tag="total_t", name="inv_length")
-            for b in range(NB):
+
+        def normalise(k, first_block, n_blocks):
+            blocks = slice(first_block, first_block + n_blocks)
+            cols = slice(first_block * P, (first_block + n_blocks) * P)
+            squares = work.tile([P, n_blocks * P], BF16, name="squares")
+            nc.scalar.activation(squares[:], x_sb[k][:, cols], FN.Square)
+            length2_t = ps_total.tile([P, n_blocks], F32, tag="total_t", name="length2_t")
+            sum_over_d(length2_t, squares, n_blocks)
+            nc.scalar.activation(
+                inv_length_t[:, k, blocks], length2_t[:], FN.Abs_reciprocal_sqrt
+            )
+            inv_length = ps_total.tile([P, n_blocks * P], F32, tag="total_t", name="inv_length")
+            for b in range(n_blocks):
                 nc.tensor.transpose(
                     inv_length[:, b * P : (b + 1) * P],
-                    inv_length_t[:, k, b : b + 1].to_broadcast([P, P]),
+                    inv_length_t[:, k, first_block + b : first_block + b + 1].to_broadcast([P, P]),
                     ident[:],
                 )
-            nc.vector.tensor_tensor(xn[k][:], x_sb[k][:], inv_length[:], ALU.mult)
+            nc.vector.tensor_tensor(xn[k][:, cols], x_sb[k][:, cols], inv_length[:], ALU.mult)
+
+        for k in range(KC):
+            n_blocks = NB // 2 if k == 0 else NB
+            for first_block in range(0, NB, n_blocks):
+                normalise(k, first_block, n_blocks)
 
         sums_t = ps_held.tile([P, M, NB, KC], F32, name="sums_t")
 
@@ -95,7 +109,7 @@ def tile_disengcn_kernel(tc, x, offs, out):
                 )
                 q_bf = casts.tile([P, S], BF16, name="q_bf")
                 nc.scalar.activation(q_bf[:], q_long[:], FN.Copy)
-                sum_over_d(sums_t[:, m, :, k], q_bf)
+                sum_over_d(sums_t[:, m, :, k], q_bf, NB)
 
         p_wide = [held.tile([P, KC, S], F32, name=f"p_wide{m}") for m in range(M)]
 

@@ -65,13 +65,17 @@ def tile_disengcn_kernel(tc, x, offs, out):
         xn = [held.tile([P, S], F32, name=f"xn{k}") for k in range(KC)]
         inv_length_t = held.tile([P, KC, NB], F32, name="inv_length_t")
 
-        def normalise(k, first_block, n_blocks):
-            blocks = slice(first_block, first_block + n_blocks)
+        def lengths(k, first_block, n_blocks):
             cols = slice(first_block * P, (first_block + n_blocks) * P)
             squares = work.tile([P, n_blocks * P], BF16, name="squares")
             nc.scalar.activation(squares[:], x_sb[k][:, cols], FN.Square)
             length2_t = ps_total.tile([P, n_blocks], F32, tag="total_t", name="length2_t")
             sum_over_d(length2_t, squares, n_blocks)
+            return length2_t
+
+        def window(k, first_block, n_blocks, length2_t):
+            blocks = slice(first_block, first_block + n_blocks)
+            cols = slice(first_block * P, (first_block + n_blocks) * P)
             nc.scalar.activation(
                 inv_length_t[:, k, blocks], length2_t[:], FN.Abs_reciprocal_sqrt
             )
@@ -84,10 +88,13 @@ def tile_disengcn_kernel(tc, x, offs, out):
                 )
             nc.vector.tensor_tensor(xn[k][:, cols], x_sb[k][:, cols], inv_length[:], ALU.mult)
 
-        for k in range(KC):
-            n_blocks = NB // 2 if k == 0 else NB
-            for first_block in range(0, NB, n_blocks):
-                normalise(k, first_block, n_blocks)
+        units = [(0, first_block, NB // 2) for first_block in range(0, NB, NB // 2)]
+        units.extend((k, 0, NB) for k in range(1, KC))
+        length2_t = lengths(*units[0])
+        for u in range(len(units)):
+            following = lengths(*units[u + 1]) if u + 1 < len(units) else None
+            window(*units[u], length2_t)
+            length2_t = following
 
         sums_t = ps_held.tile([P, M, NB, KC], F32, name="sums_t")
 

@@ -68,7 +68,10 @@ def tile_disengcn_kernel(tc, x, offs, out):
         def lengths(k, first_block, n_blocks):
             cols = slice(first_block * P, (first_block + n_blocks) * P)
             squares = work.tile([P, n_blocks * P], BF16, name="squares")
-            nc.scalar.activation(squares[:], x_sb[k][:, cols], FN.Square)
+            if k == 1:
+                nc.vector.tensor_tensor(squares[:], x_sb[k][:, cols], x_sb[k][:, cols], ALU.mult)
+            else:
+                nc.scalar.activation(squares[:], x_sb[k][:, cols], FN.Square)
             length2_t = ps_total.tile([P, n_blocks], F32, tag="total_t", name="length2_t")
             sum_over_d(length2_t, squares, n_blocks)
             return length2_t

@@ -16,7 +16,11 @@ M = 4
 NB = S // P
 COLS = S // 16
 PSUM_BANKS = 8
-EARLY = PSUM_BANKS - 2
+ROWS = KC
+ROW_BANKS = 2
+EARLY = 6
+GROUP = EARLY // 2
+BY_VECTOR = KC // 2
 N_PRODUCTS = 3
 
 FLOPS = 3 * KC * P * S + 4 * KC * P * M * S + 3 * KC * M * S
@@ -31,7 +35,9 @@ def tile_disengcn_kernel(tc, x, offs, out):
         held = ctx.enter_context(tc.tile_pool(name="held", bufs=1))
         work = ctx.enter_context(tc.tile_pool(name="work", bufs=2))
         casts = ctx.enter_context(tc.tile_pool(name="casts", bufs=N_PRODUCTS))
-        ps_total = ctx.enter_context(tc.psum_pool(name="ps_total", bufs=EARLY))
+        banks = ctx.enter_context(tc.psum_pool(name="banks", bufs=PSUM_BANKS - 1 - ROW_BANKS))
+        row_banks = ctx.enter_context(tc.psum_pool(name="row_banks", bufs=ROW_BANKS))
+        rows = ctx.enter_context(tc.tile_pool(name="rows", bufs=ROWS))
         ps_held = ctx.enter_context(tc.psum_pool(name="ps_held", bufs=1))
 
         offsets = held.tile([P, M * COLS], U16, name="offsets")
@@ -72,17 +78,20 @@ def tile_disengcn_kernel(tc, x, offs, out):
                 nc.vector.tensor_tensor(squares[:], x_sb[k][:, cols], x_sb[k][:, cols], ALU.mult)
             else:
                 nc.scalar.activation(squares[:], x_sb[k][:, cols], FN.Square)
-            length2_t = ps_total.tile([P, n_blocks], F32, tag="total_t", name="length2_t")
+            length2_t = banks.tile([P, n_blocks], F32, tag="bank", name="length2_t")
             sum_over_d(length2_t, squares, n_blocks)
             return length2_t
 
-        def window(k, first_block, n_blocks, length2_t):
+        def inverse_lengths(k, first_block, n_blocks, length2_t):
             blocks = slice(first_block, first_block + n_blocks)
-            cols = slice(first_block * P, (first_block + n_blocks) * P)
             nc.scalar.activation(
                 inv_length_t[:, k, blocks], length2_t[:], FN.Abs_reciprocal_sqrt
             )
-            inv_length = ps_total.tile([P, n_blocks * P], F32, tag="total_t", name="inv_length")
+
+        def window(k, first_block, n_blocks, length2_t):
+            cols = slice(first_block * P, (first_block + n_blocks) * P)
+            inverse_lengths(k, first_block, n_blocks, length2_t)
+            inv_length = banks.tile([P, n_blocks * P], F32, tag="bank", name="inv_length")
             for b in range(n_blocks):
                 nc.tensor.transpose(
                     inv_length[:, b * P : (b + 1) * P],
@@ -91,13 +100,32 @@ def tile_disengcn_kernel(tc, x, offs, out):
                 )
             nc.vector.tensor_tensor(xn[k][:, cols], x_sb[k][:, cols], inv_length[:], ALU.mult)
 
+        def turn_and_scale(k, length2_t):
+            inverse_lengths(k, 0, NB, length2_t)
+            x_t = banks.tile([P, NB, P], F32, tag="bank", name="x_t")
+            for b in range(NB):
+                nc.tensor.transpose(x_t[:, b, :], x_sb[k][:, b * P : (b + 1) * P], ident[:])
+            xn_t = work.tile([P, NB, P], F32, name="xn_t")
+            for b in range(NB):
+                nc.scalar.activation(
+                    xn_t[:, b, :], x_t[:, b, :], FN.Copy, scale=inv_length_t[:, k, b : b + 1]
+                )
+            return xn_t
+
+        def turn_window_back(k, xn_t):
+            xn_back = banks.tile([P, S], F32, tag="bank", name="xn_back")
+            for b in range(NB):
+                nc.tensor.transpose(xn_back[:, b * P : (b + 1) * P], xn_t[:, b, :], ident[:])
+            nc.scalar.activation(xn[k][:], xn_back[:], FN.Copy)
+
         units = [(0, first_block, NB // 2) for first_block in range(0, NB, NB // 2)]
-        units.extend((k, 0, NB) for k in range(1, KC))
+        units.extend((k, 0, NB) for k in range(1, BY_VECTOR))
         length2_t = lengths(*units[0])
         for u in range(len(units)):
-            following = lengths(*units[u + 1]) if u + 1 < len(units) else None
+            following = units[u + 1] if u + 1 < len(units) else (BY_VECTOR, 0, NB)
+            following_length2_t = lengths(*following)
             window(*units[u], length2_t)
-            length2_t = following
+            length2_t = following_length2_t
 
         sums_t = ps_held.tile([P, M, NB, KC], F32, name="sums_t")
 
@@ -111,17 +139,21 @@ def tile_disengcn_kernel(tc, x, offs, out):
         def piece(m):
             return offsets[:, m * COLS : (m + 1) * COLS]
 
-        def agreements(m):
-            for k in range(KC):
-                q_long = next_product()
-                nc.vector.tensor_tensor(
-                    q_long[:], xn[k][:].indirect(piece(m)), x_sb[k][:], ALU.mult
-                )
-                q_bf = casts.tile([P, S], BF16, name="q_bf")
-                nc.scalar.activation(q_bf[:], q_long[:], FN.Copy)
-                sum_over_d(sums_t[:, m, :, k], q_bf, NB)
+        def agreement(m, k):
+            q_long = next_product()
+            nc.vector.tensor_tensor(
+                q_long[:], xn[k][:].indirect(piece(m)), x_sb[k][:], ALU.mult
+            )
+            q_bf = casts.tile([P, S], BF16, name="q_bf")
+            nc.scalar.activation(q_bf[:], q_long[:], FN.Copy)
+            sum_over_d(sums_t[:, m, :, k], q_bf, NB)
+            if len(p_wide) < ROWS:
+                spread_next()
 
-        p_wide = [held.tile([P, KC, S], F32, name=f"p_wide{m}") for m in range(M)]
+        p_wide = {}
+
+        p_t_of = {}
+        to_spread = []
 
         def softmax(m):
             a_t = work.tile([P, NB, KC], F32, name="a_t")
@@ -136,23 +168,28 @@ def tile_disengcn_kernel(tc, x, offs, out):
                 )
             inv_den_t = work.tile([P, NB], F32, name="inv_den_t")
             nc.vector.reciprocal(inv_den_t[:], den_t[:])
-            p_t = work.tile([P, NB, KC], F32, name="p_t")
+            p_t = held.tile([P, NB, KC], F32, name=f"p_t{m}")
             for b in range(NB):
                 nc.scalar.activation(
                     p_t[:, b, :], e_t[:, b, :], FN.Copy, scale=inv_den_t[:, b : b + 1]
                 )
-            p_back = ps_held.tile([KC, S], F32, tag="short", name="p_back")
-            for b in range(NB):
-                nc.tensor.transpose(p_back[:, b * P : (b + 1) * P], p_t[:, b, :], ident[:])
-            p_rows = work.tile([KC, S], F32, name="p_rows")
-            nc.scalar.activation(p_rows[:], p_back[:], FN.Copy)
-            first_row = (KC - 1) * P + m * KC
-            parked = out[first_row : first_row + KC, :]
-            nc.sync.dma_start(parked, p_rows[:])
-            nc.sync.dma_start(
-                p_wide[m][:].rearrange("d k s -> d (k s)"),
-                parked.rearrange("k s -> (k s)").partition_broadcast(P),
-            )
+            p_t_of[m] = p_t
+            to_spread.extend((k // GROUP, m, k) for k in range(KC))
+            to_spread[:] = sorted(to_spread)
+
+        def spread_next():
+            if to_spread:
+                group, m, k = to_spread[0]
+                to_spread.remove((group, m, k))
+                row = row_banks.tile([P, S], F32, name="row")
+                for b in range(NB):
+                    nc.tensor.transpose(
+                        row[:, b * P : (b + 1) * P],
+                        p_t_of[m][:, b, k : k + 1].to_broadcast([P, P]),
+                        ident[:],
+                    )
+                p_wide[m, k] = rows.tile([P, S], F32, name="p_wide")
+                nc.scalar.activation(p_wide[m, k][:], row[:], FN.Copy)
 
         total_t = {}
 
@@ -167,10 +204,6 @@ def tile_disengcn_kernel(tc, x, offs, out):
                     stop=(last and b == NB - 1),
                 )
 
-        def open_total(k):
-            total_t[k] = ps_total.tile([P, NB, P], F32, name="total_t")
-            add_to_total(k, xn[k], True, False)
-
         def turn_back(k, turned):
             result_t = work.tile([P, NB, P], F32, name="result_t")
             nc.scalar.activation(result_t[:], total_t[k][:], FN.Copy)
@@ -179,30 +212,50 @@ def tile_disengcn_kernel(tc, x, offs, out):
 
         def weighted(m, k):
             z_p = next_product()
-            nc.vector.tensor_tensor(z_p[:], xn[k][:].indirect(piece(m)), p_wide[m][:, k, :], ALU.mult)
+            nc.vector.tensor_tensor(z_p[:], xn[k][:].indirect(piece(m)), p_wide[m, k][:], ALU.mult)
+            spread_next()
             return z_p
 
-        for k in range(EARLY):
-            open_total(k)
-        for m in range(M):
-            agreements(m)
+        def add_products(m, k, last_m):
+            if m == 0:
+                total_t[k] = banks.tile([P, NB, P], F32, tag="bank", name="total_t")
+            add_to_total(k, weighted(m, k), m == 0, m == last_m)
+            if m == 0:
+                add_to_total(k, xn[k], False, False)
+
+        for k in range(BY_VECTOR):
+            made = k + BY_VECTOR
+            agreement(0, k)
+            xn_t = turn_and_scale(made, length2_t)
+            if made + 1 < KC:
+                length2_t = lengths(made + 1, 0, NB)
+            agreement(1, k)
+            turn_window_back(made, xn_t)
+        for m in range(M // 2):
+            for k in range(BY_VECTOR, KC):
+                agreement(m, k)
             softmax(m)
-        for m in range(M):
-            for k in range(EARLY):
-                add_to_total(k, weighted(m, k), False, m == M - 1)
-                if m == M - 1:
-                    turned = ps_held.tile([P, S], F32, tag="short", name="turned")
-                    turn_back(k, turned)
-                    result = work.tile([P, S], F32, name="result")
-                    nc.scalar.activation(result[:], turned[:], FN.Copy)
-                    nc.sync.dma_start(out_caps[k], result[:])
+        for m in range(M // 2, M):
+            for k in range(KC):
+                agreement(m, k)
+            softmax(m)
         late = range(EARLY, KC)
+        for first in range(0, EARLY, GROUP):
+            group = range(first, first + GROUP)
+            for m in range(M):
+                for k in group:
+                    add_products(m, k, M - 1)
+            for k in group:
+                turned = banks.tile([P, S], F32, tag="bank", name="turned")
+                turn_back(k, turned)
+                result = work.tile([P, S], F32, name="result")
+                nc.scalar.activation(result[:], turned[:], FN.Copy)
+                nc.sync.dma_start(out_caps[k], result[:])
         all_but_last = {}
         for k in late:
-            open_total(k)
             for m in range(M - 1):
-                add_to_total(k, weighted(m, k), False, m == M - 2)
-            all_but_last[k] = ps_total.tile([P, S], F32, tag="total_t", name="all_but_last")
+                add_products(m, k, M - 2)
+            all_but_last[k] = banks.tile([P, S], F32, tag="bank", name="all_but_last")
             turn_back(k, all_but_last[k])
         for k in late:
             finished = work.tile([P, S], F32, name="finished")

@@ -21,7 +21,7 @@ ROW_BANKS = 2
 EARLY = 6
 GROUP = EARLY // 2
 BY_VECTOR = KC // 2
-N_PRODUCTS = 3
+N_PRODUCTS = 4
 
 FLOPS = 3 * KC * P * S + 4 * KC * P * M * S + 3 * KC * M * S
 
@@ -210,9 +210,15 @@ def tile_disengcn_kernel(tc, x, offs, out):
             for b in range(NB):
                 nc.tensor.transpose(turned[:, b * P : (b + 1) * P], result_t[:, b, :], ident[:])
 
-        def weighted(m, k):
+        def weighted(m, k, first=0, n=S):
             z_p = next_product()
-            nc.vector.tensor_tensor(z_p[:], xn[k][:].indirect(piece(m)), p_wide[m, k][:], ALU.mult)
+            column = (m * S + first) // 16
+            nc.vector.tensor_tensor(
+                z_p[:, :n],
+                xn[k][:].indirect(offsets[:, column : column + n // 16]),
+                p_wide[m, k][:, first : first + n],
+                ALU.mult,
+            )
             spread_next()
             return z_p
 
@@ -257,9 +263,18 @@ def tile_disengcn_kernel(tc, x, offs, out):
                 add_products(m, k, M - 2)
             all_but_last[k] = banks.tile([P, S], F32, tag="bank", name="all_but_last")
             turn_back(k, all_but_last[k])
-        for k in late:
-            finished = work.tile([P, S], F32, name="finished")
+
+        def finish(k, z_p, first, n):
+            finished = work.tile([P, n], F32, name=f"finished{n}")
             nc.vector.tensor_tensor(
-                finished[:], weighted(M - 1, k)[:], all_but_last[k][:], ALU.add
+                finished[:], z_p[:, :n], all_but_last[k][:, first : first + n], ALU.add
             )
-            nc.sync.dma_start(out_caps[k], finished[:])
+            nc.sync.dma_start(out_caps[k][:, first : first + n], finished[:])
+
+        last_half = S // 2
+        products_6 = weighted(M - 1, KC - 2)
+        products_7 = weighted(M - 1, KC - 1, 0, last_half)
+        finish(KC - 2, products_6, 0, S)
+        products_7b = weighted(M - 1, KC - 1, last_half, last_half)
+        finish(KC - 1, products_7, 0, last_half)
+        finish(KC - 1, products_7b, last_half, last_half)

@@ -21,7 +21,7 @@ ROW_BANKS = 2
 EARLY = 6
 GROUP = EARLY // 2
 BY_VECTOR = KC // 2
-N_PRODUCTS = 4
+N_PRODUCTS = 5
 
 FLOPS = 3 * KC * P * S + 4 * KC * P * M * S + 3 * KC * M * S
 

from contextlib import ExitStack

import concourse.mybir as mybir
from concourse.masks import make_identity

F32 = mybir.dt.float32
BF16 = mybir.dt.bfloat16
U16 = mybir.dt.uint16
FN = mybir.ActivationFunctionType
ALU = mybir.AluOpType

P = 128
KC = 8
S = 512
M = 4
NB = S // P
COLS = S // 16
PSUM_BANKS = 8
ROWS = KC
ROW_BANKS = 2
EARLY = 6
GROUP = EARLY // 2
BY_VECTOR = KC // 2
N_PRODUCTS = 5

FLOPS = 3 * KC * P * S + 4 * KC * P * M * S + 3 * KC * M * S


def tile_disengcn_kernel(tc, x, offs, out):
    nc = tc.nc
    x_caps = x.rearrange("(k d) s -> k d s", d=P)
    out_caps = out.rearrange("(k d) s -> k d s", d=P)

    with ExitStack() as ctx:
        held = ctx.enter_context(tc.tile_pool(name="held", bufs=1))
        work = ctx.enter_context(tc.tile_pool(name="work", bufs=2))
        casts = ctx.enter_context(tc.tile_pool(name="casts", bufs=N_PRODUCTS))
        banks = ctx.enter_context(tc.psum_pool(name="banks", bufs=PSUM_BANKS - 1 - ROW_BANKS))
        row_banks = ctx.enter_context(tc.psum_pool(name="row_banks", bufs=ROW_BANKS))
        rows = ctx.enter_context(tc.tile_pool(name="rows", bufs=ROWS))
        ps_held = ctx.enter_context(tc.psum_pool(name="ps_held", bufs=1))

        offsets = held.tile([P, M * COLS], U16, name="offsets")
        x_sb = [held.tile([P, S], F32, name=f"x{k}") for k in range(KC)]
        for first in range(0, S, S // 2):
            nc.sync.dma_start(
                x_sb[0][:, first : first + S // 2], x_caps[0][:, first : first + S // 2]
            )
        nc.sync.dma_start(offsets[:], offs)
        for k in range(1, KC):
            nc.sync.dma_start(x_sb[k][:], x_caps[k])

        warm = held.tile([P, 1], F32, name="warm")
        nc.vector.memset(warm[:], 1.0)
        nc.scalar.activation(warm[:], warm[:], FN.Abs_reciprocal_sqrt)
        ones = held.tile([P, 1], BF16, name="ones")
        nc.vector.memset(ones[:], 1.0)
        ident = held.tile([P, P], F32, name="ident")
        make_identity(nc, ident[:])

        def sum_over_d(dest, values, n_blocks):
            for b in range(n_blocks):
                nc.tensor.matmul(
                    dest[:, b : b + 1],
                    values[:, b * P : (b + 1) * P],
                    ones[:],
                    start=True,
                    stop=True,
                )

        xn = [held.tile([P, S], F32, name=f"xn{k}") for k in range(KC)]
        inv_length_t = held.tile([P, KC, NB], F32, name="inv_length_t")

        def lengths(k, first_block, n_blocks):
            cols = slice(first_block * P, (first_block + n_blocks) * P)
            squares = work.tile([P, n_blocks * P], BF16, name="squares")
            if k == 1:
                nc.vector.tensor_tensor(squares[:], x_sb[k][:, cols], x_sb[k][:, cols], ALU.mult)
            else:
                nc.scalar.activation(squares[:], x_sb[k][:, cols], FN.Square)
            length2_t = banks.tile([P, n_blocks], F32, tag="bank", name="length2_t")
            sum_over_d(length2_t, squares, n_blocks)
            return length2_t

        def inverse_lengths(k, first_block, n_blocks, length2_t):
            blocks = slice(first_block, first_block + n_blocks)
            nc.scalar.activation(
                inv_length_t[:, k, blocks], length2_t[:], FN.Abs_reciprocal_sqrt
            )

        def window(k, first_block, n_blocks, length2_t):
            cols = slice(first_block * P, (first_block + n_blocks) * P)
            inverse_lengths(k, first_block, n_blocks, length2_t)
            inv_length = banks.tile([P, n_blocks * P], F32, tag="bank", name="inv_length")
            for b in range(n_blocks):
                nc.tensor.transpose(
                    inv_length[:, b * P : (b + 1) * P],
                    inv_length_t[:, k, first_block + b : first_block + b + 1].to_broadcast([P, P]),
                    ident[:],
                )
            nc.vector.tensor_tensor(xn[k][:, cols], x_sb[k][:, cols], inv_length[:], ALU.mult)

        def turn_and_scale(k, length2_t):
            inverse_lengths(k, 0, NB, length2_t)
            x_t = banks.tile([P, NB, P], F32, tag="bank", name="x_t")
            for b in range(NB):
                nc.tensor.transpose(x_t[:, b, :], x_sb[k][:, b * P : (b + 1) * P], ident[:])
            xn_t = work.tile([P, NB, P], F32, name="xn_t")
            for b in range(NB):
                nc.scalar.activation(
                    xn_t[:, b, :], x_t[:, b, :], FN.Copy, scale=inv_length_t[:, k, b : b + 1]
                )
            return xn_t

        def turn_window_back(k, xn_t):
            xn_back = banks.tile([P, S], F32, tag="bank", name="xn_back")
            for b in range(NB):
                nc.tensor.transpose(xn_back[:, b * P : (b + 1) * P], xn_t[:, b, :], ident[:])
            nc.scalar.activation(xn[k][:], xn_back[:], FN.Copy)

        units = [(0, first_block, NB // 2) for first_block in range(0, NB, NB // 2)]
        units.extend((k, 0, NB) for k in range(1, BY_VECTOR))
        length2_t = lengths(*units[0])
        for u in range(len(units)):
            following = units[u + 1] if u + 1 < len(units) else (BY_VECTOR, 0, NB)
            following_length2_t = lengths(*following)
            window(*units[u], length2_t)
            length2_t = following_length2_t

        sums_t = ps_held.tile([P, M, NB, KC], F32, name="sums_t")

        products = [held.tile([P, S], F32, name=f"product{i}") for i in range(N_PRODUCTS)]
        taken = []

        def next_product():
            taken.append(products[len(taken) % N_PRODUCTS])
            return taken[-1]

        def piece(m):
            return offsets[:, m * COLS : (m + 1) * COLS]

        def agreement(m, k):
            q_long = next_product()
            nc.vector.tensor_tensor(
                q_long[:], xn[k][:].indirect(piece(m)), x_sb[k][:], ALU.mult
            )
            q_bf = casts.tile([P, S], BF16, name="q_bf")
            nc.scalar.activation(q_bf[:], q_long[:], FN.Copy)
            sum_over_d(sums_t[:, m, :, k], q_bf, NB)
            if len(p_wide) < ROWS:
                spread_next()

        p_wide = {}

        p_t_of = {}
        to_spread = []

        def softmax(m):
            a_t = work.tile([P, NB, KC], F32, name="a_t")
            nc.vector.tensor_tensor(
                a_t[:], sums_t[:, m], inv_length_t[:].rearrange("p k b -> p b k"), ALU.mult
            )
            e_t = work.tile([P, NB, KC], F32, name="e_t")
            den_t = work.tile([P, NB], F32, name="den_t")
            for b in range(NB):
                nc.scalar.activation(
                    e_t[:, b, :], a_t[:, b, :], FN.Exp, accum_out=den_t[:, b : b + 1]
                )
            inv_den_t = work.tile([P, NB], F32, name="inv_den_t")
            nc.vector.reciprocal(inv_den_t[:], den_t[:])
            p_t = held.tile([P, NB, KC], F32, name=f"p_t{m}")
            for b in range(NB):
                nc.scalar.activation(
                    p_t[:, b, :], e_t[:, b, :], FN.Copy, scale=inv_den_t[:, b : b + 1]
                )
            p_t_of[m] = p_t
            to_spread.extend((k // GROUP, m, k) for k in range(KC))
            to_spread[:] = sorted(to_spread)

        def spread_next():
            if to_spread:
                group, m, k = to_spread[0]
                to_spread.remove((group, m, k))
                row = row_banks.tile([P, S], F32, name="row")
                for b in range(NB):
                    nc.tensor.transpose(
                        row[:, b * P : (b + 1) * P],
                        p_t_of[m][:, b, k : k + 1].to_broadcast([P, P]),
                        ident[:],
                    )
                p_wide[m, k] = rows.tile([P, S], F32, name="p_wide")
                nc.scalar.activation(p_wide[m, k][:], row[:], FN.Copy)

        total_t = {}

        def add_to_total(k, values, first, last):
            for b in range(NB):
                nc.tensor.matmul(
                    total_t[k][:, b, :],
                    values[:, b * P : (b + 1) * P],
                    ident[:],
                    is_transpose=True,
                    start=(first and b == 0),
                    stop=(last and b == NB - 1),
                )

        def turn_back(k, turned):
            result_t = work.tile([P, NB, P], F32, name="result_t")
            nc.scalar.activation(result_t[:], total_t[k][:], FN.Copy)
            for b in range(NB):
                nc.tensor.transpose(turned[:, b * P : (b + 1) * P], result_t[:, b, :], ident[:])

        def weighted(m, k, first=0, n=S):
            z_p = next_product()
            column = (m * S + first) // 16
            nc.vector.tensor_tensor(
                z_p[:, :n],
                xn[k][:].indirect(offsets[:, column : column + n // 16]),
                p_wide[m, k][:, first : first + n],
                ALU.mult,
            )
            spread_next()
            return z_p

        def add_products(m, k, last_m):
            if m == 0:
                total_t[k] = banks.tile([P, NB, P], F32, tag="bank", name="total_t")
            add_to_total(k, weighted(m, k), m == 0, m == last_m)
            if m == 0:
                add_to_total(k, xn[k], False, False)

        for k in range(BY_VECTOR):
            made = k + BY_VECTOR
            agreement(0, k)
            xn_t = turn_and_scale(made, length2_t)
            if made + 1 < KC:
                length2_t = lengths(made + 1, 0, NB)
            agreement(1, k)
            turn_window_back(made, xn_t)
        for m in range(M // 2):
            for k in range(BY_VECTOR, KC):
                agreement(m, k)
            softmax(m)
        for m in range(M // 2, M):
            for k in range(KC):
                agreement(m, k)
            softmax(m)
        late = range(EARLY, KC)
        for first in range(0, EARLY, GROUP):
            group = range(first, first + GROUP)
            for m in range(M):
                for k in group:
                    add_products(m, k, M - 1)
            for k in group:
                turned = banks.tile([P, S], F32, tag="bank", name="turned")
                turn_back(k, turned)
                result = work.tile([P, S], F32, name="result")
                nc.scalar.activation(result[:], turned[:], FN.Copy)
                nc.sync.dma_start(out_caps[k], result[:])
        all_but_last = {}
        for k in late:
            for m in range(M - 1):
                add_products(m, k, M - 2)
            all_but_last[k] = banks.tile([P, S], F32, tag="bank", name="all_but_last")
            turn_back(k, all_but_last[k])

        def finish(k, z_p, first, n):
            finished = work.tile([P, n], F32, name=f"finished{n}")
            nc.vector.tensor_tensor(
                finished[:], z_p[:, :n], all_but_last[k][:, first : first + n], ALU.add
            )
            nc.sync.dma_start(out_caps[k][:, first : first + n], finished[:])

        last_half = S // 2
        products_6 = weighted(M - 1, KC - 2)
        products_7 = weighted(M - 1, KC - 1, 0, last_half)
        finish(KC - 2, products_6, 0, S)
        products_7b = weighted(M - 1, KC - 1, last_half, last_half)
        finish(KC - 1, products_7, 0, last_half)
        finish(KC - 1, products_7b, last_half, last_half)
